import numpy as np
import ml_dtypes


def mxq(x, axis, fmt="e4m3"):
    dtype, down = {"e4m3": (ml_dtypes.float8_e4m3fn, 7), "e5m2": (ml_dtypes.float8_e5m2, 14)}[fmt]
    v = np.moveaxis(np.asarray(x, np.float32).astype(ml_dtypes.bfloat16).astype(np.float64), axis, -1)
    blocks = v.reshape(v.shape[:-1] + (-1, 32))
    amax = np.abs(blocks).max(-1, keepdims=True)
    byte = np.maximum(np.where(amax > 0, np.frexp(amax)[1] - 1 + 127, 0) - down, 1)
    scale = np.exp2(byte - 127.0)
    codes = (blocks / scale).astype(np.float32).astype(dtype).astype(np.float64)
    return np.moveaxis((codes * scale).reshape(v.shape), -1, axis)


WIDE = False


def mx_kscale(k):
    if not WIDE:
        return np.ones(k)
    levels = np.array([20, -20, 10, -10, 0])
    a = np.random.permutation(np.resize(levels, k // 512 * 4)).reshape(k // 512, 4)
    idx = np.arange(k)
    return np.exp2(a[idx // 512, idx % 128 // 32])


BF16 = ml_dtypes.bfloat16


def bf(x):
    return np.asarray(x, np.float32).astype(BF16)


def f64(x):
    return np.asarray(x).astype(np.float64)


B, R, CIN, N_CAPS, COUT = 2048, 128, 8, 32, 16
K = R * CIN
KC = N_CAPS * COUT


def setup_inputs():
    u = mx_kscale(KC).reshape(N_CAPS, COUT)[:, :1]
    x = bf(np.random.standard_normal((B, R, CIN)))
    W0 = bf(np.random.standard_normal((N_CAPS, R, CIN, COUT)) * np.sqrt(3.0 * R / (CIN * COUT)))
    g = bf(np.random.standard_normal((N_CAPS, B, 1, 1, COUT))
           * np.exp2(np.random.randint(-12, 1, (1, B, 1, 1, 1))) * 128.0
           * u.reshape(N_CAPS, 1, 1, 1, 1))
    s = (f64(x).reshape(B, K) @ f64(W0).reshape(N_CAPS, K, COUT)) / R
    W = bf(f64(W0) / u.reshape(N_CAPS, 1, 1, 1))
    return {"x": x, "W": W, "s": np.asarray(s, np.float32), "grad_out": g}


def reference(x, W, s, grad_out):
    sf = f64(s)
    g = f64(grad_out).reshape(N_CAPS, B, COUT)
    q = np.sum(sf * sf, axis=-1, keepdims=True)
    rq = np.sqrt(q)
    dot = np.sum(g * sf, axis=-1, keepdims=True)
    ds = rq / (1.0 + q) * g + (1.0 - q) / (rq * (1.0 + q) ** 2) * dot * sf
    dsm = ds.transpose(1, 0, 2).reshape(B, KC)
    wm = f64(W).transpose(0, 3, 1, 2).reshape(KC, K)
    gx = (1.0 / R) * (mxq(dsm, 1, "e5m2") @ mxq(wm, 0, "e4m3"))
    return gx.reshape(B, R, CIN)

@@ -1,0 +1,303 @@
+from contextlib import ExitStack
+
+import concourse.bass as bass
+import concourse.mybir as mybir
+import concourse.tile as tile
+from concourse.masks import make_identity
+
+F32 = mybir.dt.float32
+BF16 = mybir.dt.bfloat16
+U32 = mybir.dt.uint32
+U8 = mybir.dt.uint8
+E5M2_X4 = mybir.dt.float8_e5m2_x4
+E4M3_X4 = mybir.dt.float8_e4m3fn_x4
+ALU = mybir.AluOpType
+ACT = mybir.ActivationFunctionType
+AXIS = mybir.AxisListType
+
+P = 128
+PACK = 4
+BATCH = 2048
+CAPS = 32
+COUT = 16
+WIDTH = 1024
+CAPS_T = CAPS // PACK
+BS = P // PACK
+CHUNKS = 4
+ROWS = BATCH // BS // CHUNKS
+PAIRS = CAPS_T * ROWS
+KJ = WIDTH // BS
+N_MOVE = 512
+
+FLOPS = 2 * BATCH * CAPS * COUT * WIDTH
+BYTES = 2 * CAPS * WIDTH * COUT + 4 * CAPS * BATCH * COUT + 2 * CAPS * BATCH * COUT + 4 * BATCH * WIDTH
+
+
+def tile_capsulelayer_t_v_kernel(tc, x, W, s, grad_out, out):
+    nc = tc.nc
+    s_view = s.rearrange("(t n) (bs c bq) o -> t c bs n (bq o)", t=PACK, bs=BS, c=CHUNKS)
+    g_view = grad_out.rearrange("(t n) (bs c bq) x y o -> t c bs n (bq x y o)", t=PACK, bs=BS, c=CHUNKS)
+    w_view = W.rearrange("(t n) (ks kr) i o -> t ks n (kr i o)", t=PACK, ks=BS)
+    out_view = out.rearrange("(bs c bl ql) r i -> c bl bs (ql r i)", bs=BS, c=CHUNKS, bl=PACK)
+
+    with ExitStack() as ctx:
+        ctx.enter_context(tc.manual_schedule())
+        const = ctx.enter_context(tc.tile_pool(name="const", bufs=1))
+        inputs = ctx.enter_context(tc.tile_pool(name="inputs", bufs=CHUNKS))
+        work = ctx.enter_context(tc.tile_pool(name="work", bufs=3))
+        small = ctx.enter_context(tc.tile_pool(name="small", bufs=2))
+        results = ctx.enter_context(tc.tile_pool(name="results", bufs=2))
+        psum_bank = ctx.enter_context(tc.psum_pool(name="psum_bank", bufs=2))
+        psum_q = ctx.enter_context(tc.psum_pool(name="psum_q", bufs=1))
+        psum_ds = ctx.enter_context(tc.psum_pool(name="psum_ds", bufs=2))
+        psum_acc = ctx.enter_context(tc.psum_pool(name="psum_acc", bufs=3))
+
+        w_rows = const.tile([P, CAPS_T, KJ * COUT], BF16)
+        s_tiles = []
+        g_tiles = []
+        for c in range(CHUNKS):
+            if c == 1:
+                for t in range(PACK):
+                    nc.sync.dma_start(out=w_rows[t:P:PACK, :, :], in_=w_view[t])
+            s_c = inputs.tile([P, CAPS_T, ROWS * COUT], F32, name="s_c")
+            g_c = inputs.tile([P, CAPS_T, ROWS * COUT], BF16, name="g_c")
+            for t in range(PACK):
+                nc.sync.dma_start(out=s_c[t:P:PACK, :, :], in_=s_view[t, c])
+            for t in range(PACK):
+                nc.sync.dma_start(out=g_c[t:P:PACK, :, :], in_=g_view[t, c])
+            s_tiles.append(s_c)
+            g_tiles.append(g_c)
+
+        ident = const.tile([P, P], BF16)
+        make_identity(nc, ident[:])
+        ident_f32 = const.tile([P, P], F32)
+        make_identity(nc, ident_f32[:])
+        group_sum = const.tile([P, P // COUT], F32)
+        nc.vector.tensor_reduce(
+            out=group_sum[:], in_=ident_f32[:].rearrange("p (j o) -> p j o", o=COUT), axis=AXIS.X, op=ALU.add
+        )
+
+
+        q_of = {}
+        root_of = {}
+        gs_of = {}
+        dot_of = {}
+        a_of = {}
+        cf_of = {}
+        neg_of = {}
+        ds_of = {}
+        grouped_of = {}
+        acc_of = {}
+        gx_of = {}
+        BLOCKS = 4
+        BANKS = CAPS_T * ROWS * COUT // (BLOCKS * P)
+
+        def squares(c):
+            s_flat = s_tiles[c][:].rearrange("p n f -> p (n f)")
+            q = psum_q.tile([P, PAIRS], F32, name="q")
+            squared = []
+            for step in range(BANKS + 1):
+                if step < BANKS:
+                    s_t = psum_bank.tile([P, BLOCKS, P], F32, tag="bank", name="s_t")
+                    for i in range(BLOCKS):
+                        block = BLOCKS * step + i
+                        nc.tensor.transpose(
+                            out=s_t[:, i, :], in_=s_flat[:, block * P : (block + 1) * P], identity=ident_f32[:]
+                        )
+                    sq_t = work.tile([P, BLOCKS, P], F32, name="sq_t")
+                    nc.scalar.activation(out=sq_t[:], in_=s_t[:], func=ACT.Square)
+                    squared.append(sq_t)
+                if step >= 1:
+                    for i in range(BLOCKS):
+                        block = BLOCKS * (step - 1) + i
+                        nc.tensor.matmul(
+                            out=q[:, block * 8 : (block + 1) * 8],
+                            lhsT=squared[step - 1][:, i, :],
+                            rhs=group_sum[:],
+                            start=True,
+                            stop=True,
+                        )
+            root = small.tile([P, PAIRS], F32, name="root")
+            nc.scalar.sqrt(out=root[:], in_=q[:])
+            q_of[c] = q
+            root_of[c] = root
+
+        def products(c, engine):
+            gs = work.tile([P, PAIRS, COUT], F32, name="gs")
+            engine.tensor_tensor(
+                out=gs[:],
+                in0=g_tiles[c][:].rearrange("p n (bq o) -> p (n bq) o", o=COUT),
+                in1=s_tiles[c][:].rearrange("p n (bq o) -> p (n bq) o", o=COUT),
+                op=ALU.mult,
+            )
+            gs_of[c] = gs
+
+        def dots(c):
+            dot = small.tile([P, PAIRS], F32, name="dot")
+            nc.vector.tensor_reduce(out=dot[:], in_=gs_of[c][:], axis=AXIS.X, op=ALU.add)
+            dot_of[c] = dot
+
+        def factors_of_q(c):
+            q = q_of[c]
+            root = root_of[c]
+            den = small.tile([P, PAIRS], F32, name="den")
+            nc.vector.scalar_tensor_tensor(out=den[:], in0=q[:], scalar=1.0, in1=root[:], op0=ALU.add, op1=ALU.mult)
+            u = small.tile([P, PAIRS], F32, name="u")
+            nc.vector.reciprocal(out=u[:], in_=den[:])
+            a = small.tile([P, PAIRS], F32, name="a")
+            nc.vector.tensor_tensor(out=a[:], in0=q[:], in1=u[:], op=ALU.mult)
+            r1 = small.tile([P, PAIRS], F32, name="r1")
+            nc.vector.tensor_tensor(out=r1[:], in0=u[:], in1=root[:], op=ALU.mult)
+            neg = small.tile([P, PAIRS], F32, name="neg")
+            nc.vector.scalar_tensor_tensor(out=neg[:], in0=u[:], scalar=-1.0, in1=r1[:], op0=ALU.mult, op1=ALU.mult)
+            a_of[c] = a
+            neg_of[c] = neg
+
+        def factors_of_dot(c):
+            q = q_of[c]
+            neg = neg_of[c]
+            qd = small.tile([P, PAIRS], F32, name="qd")
+            nc.vector.scalar_tensor_tensor(out=qd[:], in0=q[:], scalar=1.0, in1=dot_of[c][:], op0=ALU.subtract, op1=ALU.mult)
+            cf = small.tile([P, PAIRS], F32, name="cf")
+            nc.vector.tensor_tensor(out=cf[:], in0=neg[:], in1=qd[:], op=ALU.mult)
+            cf_of[c] = cf
+
+        w_grouped = const.tile([P, BS, KJ, PACK], BF16, align_bytes=64)
+        w_codes = const.tile([P, WIDTH], U32, align_bytes=64)
+        w_scales = const.tile([P, WIDTH], U8, align_bytes=64)
+        KJ_BANK = 8
+
+        def turn_w():
+            w_sorted = const.tile([P, KJ, CAPS_T, COUT], BF16)
+            nc.scalar.copy(
+                out=w_sorted[:].rearrange("p kj n o -> p (kj n o)").bitcast(F32).rearrange(
+                    "p (kj n w) -> p kj n w", kj=KJ, n=CAPS_T
+                ),
+                in_=w_rows[:].rearrange("p n f -> p (n f)").bitcast(F32).rearrange(
+                    "p (n kj w) -> p kj n w", n=CAPS_T, kj=KJ
+                ),
+            )
+            for kj0 in range(0, KJ, KJ_BANK):
+                w_t = psum_bank.tile([P, KJ_BANK, P], BF16, tag="bank", name="w_t")
+                for i in range(KJ_BANK):
+                    nc.tensor.transpose(
+                        out=w_t[:, i, :],
+                        in_=w_sorted[:, kj0 + i, :, :].rearrange("p n o -> p (n o)"),
+                        identity=ident[:],
+                    )
+                nc.scalar.copy(
+                    out=w_grouped[:, :, kj0 : kj0 + KJ_BANK, :],
+                    in_=w_t[:].rearrange("p kj (ks t) -> p ks kj t", t=PACK),
+                )
+
+        def quantise_w():
+            nc.vector.quantize_mx(
+                out=w_codes[:].bitcast(E4M3_X4),
+                scales=w_scales[:],
+                in_=w_grouped[:].rearrange("p ks kj t -> p (ks kj t)"),
+            )
+
+        def scaled_rows(c, ql):
+            s_rows = s_tiles[c][:].rearrange("p n (bl ql o) -> p ql n bl o", ql=PACK, o=COUT)[:, ql]
+            g_rows = g_tiles[c][:].rearrange("p n (bl ql o) -> p ql n bl o", ql=PACK, o=COUT)[:, ql]
+            a_rows = a_of[c][:].rearrange("p (n bl ql) -> p ql n bl", n=CAPS_T, ql=PACK)[:, ql]
+            cf_rows = cf_of[c][:].rearrange("p (n bl ql) -> p ql n bl", n=CAPS_T, ql=PACK)[:, ql]
+            shape = [P, CAPS_T, PACK, COUT]
+            ag = work.tile([P, PACK, CAPS_T, COUT], F32, name="ag")
+            nc.vector.tensor_tensor(
+                out=ag[:].rearrange("p bl n o -> p n bl o"),
+                in0=g_rows,
+                in1=a_rows.unsqueeze(3).to_broadcast(shape),
+                op=ALU.mult,
+            )
+            cs = work.tile([P, PACK, CAPS_T, COUT], F32, name="cs")
+            nc.vector.tensor_tensor(
+                out=cs[:].rearrange("p bl n o -> p n bl o"),
+                in0=s_rows,
+                in1=cf_rows.unsqueeze(3).to_broadcast(shape),
+                op=ALU.mult,
+            )
+            ds = work.tile([P, PACK, CAPS_T * COUT], BF16, name="ds")
+            nc.gpsimd.tensor_tensor(
+                out=ds[:].rearrange("p bl f -> p (bl f)"),
+                in0=ag[:].rearrange("p bl n o -> p (bl n o)"),
+                in1=cs[:].rearrange("p bl n o -> p (bl n o)"),
+                op=ALU.add,
+            )
+            ds_of[(c, ql)] = ds
+
+        def turn(c, ql):
+            ds = ds_of[(c, ql)]
+            ds_t = psum_ds.tile([P, BS, PACK, PACK], BF16, name="ds_t")
+            for bl in range(PACK):
+                nc.tensor.transpose(out=ds_t[:, :, bl, :], in_=ds[:, bl, :], identity=ident[:])
+            ds_grouped = work.tile([P, PACK * P], BF16, name="ds_grouped", align_bytes=64)
+            nc.scalar.copy(out=ds_grouped[:], in_=ds_t[:].rearrange("p bs bl t -> p (bs bl t)"))
+            grouped_of[(c, ql)] = ds_grouped
+
+        def multiply(c, ql):
+            ds_codes = work.tile([P, P], U32, name="ds_codes", align_bytes=64)
+            ds_scales = work.tile([P, P], U8, name="ds_scales", align_bytes=64)
+            nc.vector.quantize_mx(out=ds_codes[:].bitcast(E5M2_X4), scales=ds_scales[:], in_=grouped_of[(c, ql)][:])
+            acc_of[(c, ql)] = []
+            for k0 in range(0, WIDTH, N_MOVE):
+                cols = slice(k0, k0 + N_MOVE)
+                acc = psum_acc.tile([P, N_MOVE], F32, name="acc")
+                nc.tensor.matmul_mx(
+                    out=acc[:],
+                    lhsT=ds_codes[:].bitcast(E5M2_X4),
+                    lhsT_scale=ds_scales[:],
+                    rhs=w_codes[:, cols].bitcast(E4M3_X4),
+                    rhs_scale=w_scales[:, cols],
+                    start=True,
+                    stop=True,
+                )
+                acc_of[(c, ql)].append(acc)
+
+        def evacuate(c, ql):
+            if ql == 0:
+                gx_of[c] = results.tile([P, PACK, WIDTH], F32, name="gx")
+            gx = gx_of[c]
+            for half in range(WIDTH // N_MOVE):
+                cols = slice(half * N_MOVE, (half + 1) * N_MOVE)
+                acc = acc_of[(c, ql)][half]
+                if ql % 2 == 1 and half == 1:
+                    nc.vector.tensor_scalar_mul(out=gx[:, ql, cols], in0=acc[:], scalar1=1.0 / P)
+                else:
+                    nc.scalar.mul(out=gx[:, ql, cols], in_=acc[:], mul=1.0 / P)
+            if ql % 2 == 1:
+                for bl in range(PACK):
+                    nc.sync.dma_start(
+                        out=out_view[c, bl][:, (ql - 1) * WIDTH : (ql + 1) * WIDTH],
+                        in_=gx[bl:P:PACK, ql - 1 : ql + 1, :].rearrange("p ql k -> p (ql k)"),
+                    )
+
+        squares(0)
+        products(0, nc.vector)
+        dots(0)
+        factors_of_q(0)
+        factors_of_dot(0)
+        turn_w()
+        QUADS = CHUNKS * PACK
+        for k in range(QUADS + 3):
+            c = k // PACK
+            ql = k % PACK
+            if k < QUADS:
+                scaled_rows(c, ql)
+            if 0 <= k - 3 < QUADS:
+                evacuate((k - 3) // PACK, (k - 3) % PACK)
+            if 0 <= k - 1 < QUADS:
+                turn((k - 1) // PACK, (k - 1) % PACK)
+            if k == 1:
+                quantise_w()
+            if 0 <= k - 2 < QUADS:
+                multiply((k - 2) // PACK, (k - 2) % PACK)
+            if c + 1 < CHUNKS:
+                if ql == 0:
+                    squares(c + 1)
+                    products(c + 1, nc.gpsimd)
+                if ql == 2:
+                    factors_of_q(c + 1)
+                if ql == 3:
+                    dots(c + 1)
+                    factors_of_dot(c + 1)

@@ -79,63 +79,65 @@ def tile_capsulelayer_t_v_kernel(tc, x, W, s, grad_out, out):
 
 
         q_of = {}
+        squared_of = {}
         root_of = {}
         gs_of = {}
         dot_of = {}
         a_of = {}
         cf_of = {}
         neg_of = {}
-        ds_of = {}
+        terms_of = {}
         grouped_of = {}
         acc_of = {}
         gx_of = {}
         BLOCKS = 4
         BANKS = CAPS_T * ROWS * COUT // (BLOCKS * P)
 
-        def squares(c):
+        def square_bank(c, bank):
             s_flat = s_tiles[c][:].rearrange("p n f -> p (n f)")
-            q = psum_q.tile([P, PAIRS], F32, name="q")
-            squared = []
-            for step in range(BANKS + 1):
-                if step < BANKS:
-                    s_t = psum_bank.tile([P, BLOCKS, P], F32, tag="bank", name="s_t")
-                    for i in range(BLOCKS):
-                        block = BLOCKS * step + i
-                        nc.tensor.transpose(
-                            out=s_t[:, i, :], in_=s_flat[:, block * P : (block + 1) * P], identity=ident_f32[:]
-                        )
-                    sq_t = work.tile([P, BLOCKS, P], F32, name="sq_t")
-                    nc.scalar.activation(out=sq_t[:], in_=s_t[:], func=ACT.Square)
-                    squared.append(sq_t)
-                if step >= 1:
-                    for i in range(BLOCKS):
-                        block = BLOCKS * (step - 1) + i
-                        nc.tensor.matmul(
-                            out=q[:, block * 8 : (block + 1) * 8],
-                            lhsT=squared[step - 1][:, i, :],
-                            rhs=group_sum[:],
-                            start=True,
-                            stop=True,
-                        )
-            root = small.tile([P, PAIRS], F32, name="root")
-            nc.scalar.sqrt(out=root[:], in_=q[:])
-            q_of[c] = q
-            root_of[c] = root
+            s_t = psum_bank.tile([P, BLOCKS, P], F32, tag="bank", name="s_t")
+            for i in range(BLOCKS):
+                block = BLOCKS * bank + i
+                nc.tensor.transpose(out=s_t[:, i, :], in_=s_flat[:, block * P : (block + 1) * P], identity=ident_f32[:])
+            sq_t = work.tile([P, BLOCKS, P], F32, name="sq_t", bufs=BANKS)
+            nc.scalar.activation(out=sq_t[:], in_=s_t[:], func=ACT.Square)
+            squared_of[(c, bank)] = sq_t
 
-        def products(c, engine):
-            gs = work.tile([P, PAIRS, COUT], F32, name="gs")
-            engine.tensor_tensor(
-                out=gs[:],
-                in0=g_tiles[c][:].rearrange("p n (bq o) -> p (n bq) o", o=COUT),
-                in1=s_tiles[c][:].rearrange("p n (bq o) -> p (n bq) o", o=COUT),
+        def sum_bank(c, bank):
+            if bank == 0:
+                q_of[c] = psum_q.tile([P, PAIRS], F32, name="q")
+            for i in range(BLOCKS):
+                block = BLOCKS * bank + i
+                nc.tensor.matmul(
+                    out=q_of[c][:, block * 8 : (block + 1) * 8],
+                    lhsT=squared_of[(c, bank)][:, i, :],
+                    rhs=group_sum[:],
+                    start=True,
+                    stop=True,
+                )
+            if bank == BANKS - 1:
+                root = small.tile([P, PAIRS], F32, name="root")
+                nc.scalar.sqrt(out=root[:], in_=q_of[c][:])
+                root_of[c] = root
+
+        HALF = PAIRS // 2
+
+        def products(c, half):
+            if half == 0:
+                gs_of[c] = work.tile([P, PAIRS, COUT], F32, name="gs", bufs=2)
+            pairs = slice(half * HALF, (half + 1) * HALF)
+            nc.vector.tensor_tensor(
+                out=gs_of[c][:, pairs, :],
+                in0=g_tiles[c][:].rearrange("p n (bq o) -> p (n bq) o", o=COUT)[:, pairs, :],
+                in1=s_tiles[c][:].rearrange("p n (bq o) -> p (n bq) o", o=COUT)[:, pairs, :],
                 op=ALU.mult,
             )
-            gs_of[c] = gs
 
-        def dots(c):
-            dot = small.tile([P, PAIRS], F32, name="dot")
-            nc.vector.tensor_reduce(out=dot[:], in_=gs_of[c][:], axis=AXIS.X, op=ALU.add)
-            dot_of[c] = dot
+        def dots(c, half):
+            if half == 0:
+                dot_of[c] = small.tile([P, PAIRS], F32, name="dot")
+            pairs = slice(half * HALF, (half + 1) * HALF)
+            nc.vector.tensor_reduce(out=dot_of[c][:, pairs], in_=gs_of[c][:, pairs, :], axis=AXIS.X, op=ALU.add)
 
         def factors_of_q(c):
             q = q_of[c]
@@ -217,20 +219,28 @@ def tile_capsulelayer_t_v_kernel(tc, x, W, s, grad_out, out):
                 in1=cf_rows.unsqueeze(3).to_broadcast(shape),
                 op=ALU.mult,
             )
-            ds = work.tile([P, PACK, CAPS_T * COUT], BF16, name="ds")
-            nc.gpsimd.tensor_tensor(
-                out=ds[:].rearrange("p bl f -> p (bl f)"),
-                in0=ag[:].rearrange("p bl n o -> p (bl n o)"),
-                in1=cs[:].rearrange("p bl n o -> p (bl n o)"),
-                op=ALU.add,
-            )
-            ds_of[(c, ql)] = ds
+            terms_of[(c, ql)] = (ag, cs)
 
         def turn(c, ql):
-            ds = ds_of[(c, ql)]
-            ds_t = psum_ds.tile([P, BS, PACK, PACK], BF16, name="ds_t")
+            ag, cs = terms_of[(c, ql)]
+            ds_t = psum_ds.tile([P, BS, PACK, PACK], F32, name="ds_t")
             for bl in range(PACK):
-                nc.tensor.transpose(out=ds_t[:, :, bl, :], in_=ds[:, bl, :], identity=ident[:])
+                nc.tensor.matmul(
+                    out=ds_t[:, :, bl, :],
+                    lhsT=ag[:, bl, :, :].rearrange("p n o -> p (n o)"),
+                    rhs=ident_f32[:],
+                    is_transpose=True,
+                    start=True,
+                    stop=False,
+                )
+                nc.tensor.matmul(
+                    out=ds_t[:, :, bl, :],
+                    lhsT=cs[:, bl, :, :].rearrange("p n o -> p (n o)"),
+                    rhs=ident_f32[:],
+                    is_transpose=True,
+                    start=False,
+                    stop=True,
+                )
             ds_grouped = work.tile([P, PACK * P], BF16, name="ds_grouped", align_bytes=64)
             nc.scalar.copy(out=ds_grouped[:], in_=ds_t[:].rearrange("p bs bl t -> p (bs bl t)"))
             grouped_of[(c, ql)] = ds_grouped
@@ -261,10 +271,7 @@ def tile_capsulelayer_t_v_kernel(tc, x, W, s, grad_out, out):
             for half in range(WIDTH // N_MOVE):
                 cols = slice(half * N_MOVE, (half + 1) * N_MOVE)
                 acc = acc_of[(c, ql)][half]
-                if ql % 2 == 1 and half == 1:
-                    nc.vector.tensor_scalar_mul(out=gx[:, ql, cols], in0=acc[:], scalar1=1.0 / P)
-                else:
-                    nc.scalar.mul(out=gx[:, ql, cols], in_=acc[:], mul=1.0 / P)
+                nc.scalar.mul(out=gx[:, ql, cols], in_=acc[:], mul=1.0 / P)
             if ql % 2 == 1:
                 for bl in range(PACK):
                     nc.sync.dma_start(
@@ -272,11 +279,21 @@ def tile_capsulelayer_t_v_kernel(tc, x, W, s, grad_out, out):
                         in_=gx[bl:P:PACK, ql - 1 : ql + 1, :].rearrange("p ql k -> p (ql k)"),
                     )
 
-        squares(0)
-        products(0, nc.vector)
-        dots(0)
-        factors_of_q(0)
-        factors_of_dot(0)
+        def prepare(c, piece):
+            if piece < 2:
+                square_bank(c, 2 * piece)
+                square_bank(c, 2 * piece + 1)
+                products(c, piece)
+            if 1 <= piece < 3:
+                sum_bank(c, 2 * piece - 2)
+                sum_bank(c, 2 * piece - 1)
+                dots(c, piece - 1)
+            if piece == 3:
+                factors_of_q(c)
+                factors_of_dot(c)
+
+        for piece in range(PACK):
+            prepare(0, piece)
         turn_w()
         QUADS = CHUNKS * PACK
         for k in range(QUADS + 3):
@@ -293,11 +310,4 @@ def tile_capsulelayer_t_v_kernel(tc, x, W, s, grad_out, out):
             if 0 <= k - 2 < QUADS:
                 multiply((k - 2) // PACK, (k - 2) % PACK)
             if c + 1 < CHUNKS:
-                if ql == 0:
-                    squares(c + 1)
-                    products(c + 1, nc.gpsimd)
-                if ql == 2:
-                    factors_of_q(c + 1)
-                if ql == 3:
-                    dots(c + 1)
-                    factors_of_dot(c + 1)
+                prepare(c + 1, ql)

@@ -28,6 +28,7 @@ ROWS = BATCH // BS // CHUNKS
 PAIRS = CAPS_T * ROWS
 KJ = WIDTH // BS
 N_MOVE = 512
+SUM_COLS = 64
 
 FLOPS = 2 * BATCH * CAPS * COUT * WIDTH
 BYTES = 2 * CAPS * WIDTH * COUT + 4 * CAPS * BATCH * COUT + 2 * CAPS * BATCH * COUT + 4 * BATCH * WIDTH
@@ -72,14 +73,19 @@ def tile_capsulelayer_t_v_kernel(tc, x, W, s, grad_out, out):
         make_identity(nc, ident[:])
         ident_f32 = const.tile([P, P], F32)
         make_identity(nc, ident_f32[:])
-        group_sum = const.tile([P, P // COUT], F32)
+        group_sum = const.tile([P, SUM_COLS], F32)
+        nc.vector.memset(group_sum[:], 0.0)
         nc.vector.tensor_reduce(
-            out=group_sum[:], in_=ident_f32[:].rearrange("p (j o) -> p j o", o=COUT), axis=AXIS.X, op=ALU.add
+            out=group_sum[:, 0 : P // COUT],
+            in_=ident_f32[:].rearrange("p (j o) -> p j o", o=COUT),
+            axis=AXIS.X,
+            op=ALU.add,
         )
 
 
         q_of = {}
         squared_of = {}
+        q_wide_of = {}
         root_of = {}
         gs_of = {}
         dot_of = {}
@@ -105,11 +111,12 @@ def tile_capsulelayer_t_v_kernel(tc, x, W, s, grad_out, out):
 
         def sum_bank(c, bank):
             if bank == 0:
-                q_of[c] = psum_q.tile([P, PAIRS], F32, name="q")
+                q_wide_of[c] = psum_q.tile([P, PAIRS + SUM_COLS - 8], F32, name="q_wide")
+                q_of[c] = q_wide_of[c][:, 0:PAIRS]
             for i in range(BLOCKS):
                 block = BLOCKS * bank + i
                 nc.tensor.matmul(
-                    out=q_of[c][:, block * 8 : (block + 1) * 8],
+                    out=q_wide_of[c][:, block * 8 : block * 8 + SUM_COLS],
                     lhsT=squared_of[(c, bank)][:, i, :],
                     rhs=group_sum[:],
                     start=True,
@@ -117,7 +124,7 @@ def tile_capsulelayer_t_v_kernel(tc, x, W, s, grad_out, out):
                 )
             if bank == BANKS - 1:
                 root = small.tile([P, PAIRS], F32, name="root")
-                nc.scalar.sqrt(out=root[:], in_=q_of[c][:])
+                nc.scalar.sqrt(out=root[:], in_=q_of[c])
                 root_of[c] = root
 
         HALF = PAIRS // 2
@@ -143,11 +150,11 @@ def tile_capsulelayer_t_v_kernel(tc, x, W, s, grad_out, out):
             q = q_of[c]
             root = root_of[c]
             den = small.tile([P, PAIRS], F32, name="den")
-            nc.vector.scalar_tensor_tensor(out=den[:], in0=q[:], scalar=1.0, in1=root[:], op0=ALU.add, op1=ALU.mult)
+            nc.vector.scalar_tensor_tensor(out=den[:], in0=q, scalar=1.0, in1=root[:], op0=ALU.add, op1=ALU.mult)
             u = small.tile([P, PAIRS], F32, name="u")
             nc.vector.reciprocal(out=u[:], in_=den[:])
             a = small.tile([P, PAIRS], F32, name="a")
-            nc.vector.tensor_tensor(out=a[:], in0=q[:], in1=u[:], op=ALU.mult)
+            nc.vector.tensor_tensor(out=a[:], in0=q, in1=u[:], op=ALU.mult)
             r1 = small.tile([P, PAIRS], F32, name="r1")
             nc.vector.tensor_tensor(out=r1[:], in0=u[:], in1=root[:], op=ALU.mult)
             neg = small.tile([P, PAIRS], F32, name="neg")
@@ -159,7 +166,7 @@ def tile_capsulelayer_t_v_kernel(tc, x, W, s, grad_out, out):
             q = q_of[c]
             neg = neg_of[c]
             qd = small.tile([P, PAIRS], F32, name="qd")
-            nc.vector.scalar_tensor_tensor(out=qd[:], in0=q[:], scalar=1.0, in1=dot_of[c][:], op0=ALU.subtract, op1=ALU.mult)
+            nc.vector.scalar_tensor_tensor(out=qd[:], in0=q, scalar=1.0, in1=dot_of[c][:], op0=ALU.subtract, op1=ALU.mult)
             cf = small.tile([P, PAIRS], F32, name="cf")
             nc.vector.tensor_tensor(out=cf[:], in0=neg[:], in1=qd[:], op=ALU.mult)
             cf_of[c] = cf
@@ -280,21 +287,23 @@ def tile_capsulelayer_t_v_kernel(tc, x, W, s, grad_out, out):
                     )
 
         def prepare(c, piece):
-            if piece < 2:
-                square_bank(c, 2 * piece)
-                square_bank(c, 2 * piece + 1)
-                products(c, piece)
+            if piece < BANKS:
+                square_bank(c, piece)
+            if 1 <= piece:
+                sum_bank(c, piece - 1)
             if 1 <= piece < 3:
-                sum_bank(c, 2 * piece - 2)
-                sum_bank(c, 2 * piece - 1)
-                dots(c, piece - 1)
+                products(c, piece - 1)
             if piece == 3:
+                dots(c, 0)
+                dots(c, 1)
+            if piece == 4:
                 factors_of_q(c)
                 factors_of_dot(c)
 
-        for piece in range(PACK):
+        for piece in range(5):
             prepare(0, piece)
         turn_w()
+        prepare(1, 0)
         QUADS = CHUNKS * PACK
         for k in range(QUADS + 3):
             c = k // PACK
@@ -310,4 +319,6 @@ def tile_capsulelayer_t_v_kernel(tc, x, W, s, grad_out, out):
             if 0 <= k - 2 < QUADS:
                 multiply((k - 2) // PACK, (k - 2) % PACK)
             if c + 1 < CHUNKS:
-                prepare(c + 1, ql)
+                prepare(c + 1, ql + 1)
+            if c + 2 < CHUNKS and ql == PACK - 1:
+                prepare(c + 2, 0)

@@ -289,27 +289,34 @@ def tile_capsulelayer_t_v_kernel(tc, x, W, s, grad_out, out):
         def prepare(c, piece):
             if piece < BANKS:
                 square_bank(c, piece)
-            if 1 <= piece:
+            if 1 <= piece <= BANKS:
                 sum_bank(c, piece - 1)
-            if 1 <= piece < 3:
-                products(c, piece - 1)
-            if piece == 3:
+            if 2 <= piece < 4:
+                products(c, piece - 2)
+            if piece == 4:
                 dots(c, 0)
                 dots(c, 1)
-            if piece == 4:
+            if piece == 5:
                 factors_of_q(c)
                 factors_of_dot(c)
 
-        for piece in range(5):
+        PIECES = 6
+        LEAD = PIECES - PACK
+        for piece in range(PIECES):
             prepare(0, piece)
         turn_w()
-        prepare(1, 0)
+        for piece in range(LEAD):
+            prepare(1, piece)
         QUADS = CHUNKS * PACK
         for k in range(QUADS + 3):
             c = k // PACK
             ql = k % PACK
             if k < QUADS:
                 scaled_rows(c, ql)
+            if c + 1 < CHUNKS:
+                prepare(c + 1, ql + LEAD)
+            if c + 2 < CHUNKS and ql >= PACK - LEAD:
+                prepare(c + 2, ql - (PACK - LEAD))
             if 0 <= k - 3 < QUADS:
                 evacuate((k - 3) // PACK, (k - 3) % PACK)
             if 0 <= k - 1 < QUADS:
@@ -318,7 +325,3 @@ def tile_capsulelayer_t_v_kernel(tc, x, W, s, grad_out, out):
                 quantise_w()
             if 0 <= k - 2 < QUADS:
                 multiply((k - 2) // PACK, (k - 2) % PACK)
-            if c + 1 < CHUNKS:
-                prepare(c + 1, ql + 1)
-            if c + 2 < CHUNKS and ql == PACK - 1:
-                prepare(c + 2, 0)

@@ -92,6 +92,9 @@ def tile_capsulelayer_t_v_kernel(tc, x, W, s, grad_out, out):
         a_of = {}
         cf_of = {}
         neg_of = {}
+        den_of = {}
+        u_of = {}
+        qd_of = {}
         terms_of = {}
         grouped_of = {}
         acc_of = {}
@@ -146,29 +149,37 @@ def tile_capsulelayer_t_v_kernel(tc, x, W, s, grad_out, out):
             pairs = slice(half * HALF, (half + 1) * HALF)
             nc.vector.tensor_reduce(out=dot_of[c][:, pairs], in_=gs_of[c][:, pairs, :], axis=AXIS.X, op=ALU.add)
 
-        def factors_of_q(c):
-            q = q_of[c]
-            root = root_of[c]
+        def factors_den(c):
             den = small.tile([P, PAIRS], F32, name="den")
-            nc.vector.scalar_tensor_tensor(out=den[:], in0=q, scalar=1.0, in1=root[:], op0=ALU.add, op1=ALU.mult)
+            nc.vector.scalar_tensor_tensor(
+                out=den[:], in0=q_of[c], scalar=1.0, in1=root_of[c][:], op0=ALU.add, op1=ALU.mult
+            )
+            den_of[c] = den
+
+        def factors_u(c):
             u = small.tile([P, PAIRS], F32, name="u")
-            nc.vector.reciprocal(out=u[:], in_=den[:])
-            a = small.tile([P, PAIRS], F32, name="a")
-            nc.vector.tensor_tensor(out=a[:], in0=q, in1=u[:], op=ALU.mult)
+            nc.vector.reciprocal(out=u[:], in_=den_of[c][:])
+            qd = small.tile([P, PAIRS], F32, name="qd")
+            nc.vector.scalar_tensor_tensor(
+                out=qd[:], in0=q_of[c], scalar=1.0, in1=dot_of[c][:], op0=ALU.subtract, op1=ALU.mult
+            )
+            u_of[c] = u
+            qd_of[c] = qd
+
+        def factors_a(c):
+            u = u_of[c]
             r1 = small.tile([P, PAIRS], F32, name="r1")
-            nc.vector.tensor_tensor(out=r1[:], in0=u[:], in1=root[:], op=ALU.mult)
+            nc.vector.tensor_tensor(out=r1[:], in0=u[:], in1=root_of[c][:], op=ALU.mult)
+            a = small.tile([P, PAIRS], F32, name="a")
+            nc.vector.tensor_tensor(out=a[:], in0=q_of[c], in1=u[:], op=ALU.mult)
             neg = small.tile([P, PAIRS], F32, name="neg")
             nc.vector.scalar_tensor_tensor(out=neg[:], in0=u[:], scalar=-1.0, in1=r1[:], op0=ALU.mult, op1=ALU.mult)
             a_of[c] = a
             neg_of[c] = neg
 
-        def factors_of_dot(c):
-            q = q_of[c]
-            neg = neg_of[c]
-            qd = small.tile([P, PAIRS], F32, name="qd")
-            nc.vector.scalar_tensor_tensor(out=qd[:], in0=q, scalar=1.0, in1=dot_of[c][:], op0=ALU.subtract, op1=ALU.mult)
+        def factors_cf(c):
             cf = small.tile([P, PAIRS], F32, name="cf")
-            nc.vector.tensor_tensor(out=cf[:], in0=neg[:], in1=qd[:], op=ALU.mult)
+            nc.vector.tensor_tensor(out=cf[:], in0=neg_of[c][:], in1=qd_of[c][:], op=ALU.mult)
             cf_of[c] = cf
 
         w_grouped = const.tile([P, BS, KJ, PACK], BF16, align_bytes=64)
@@ -279,11 +290,12 @@ def tile_capsulelayer_t_v_kernel(tc, x, W, s, grad_out, out):
                 cols = slice(half * N_MOVE, (half + 1) * N_MOVE)
                 acc = acc_of[(c, ql)][half]
                 nc.scalar.mul(out=gx[:, ql, cols], in_=acc[:], mul=1.0 / P)
-            if ql % 2 == 1:
+            first = ql if c == CHUNKS - 1 else ql - 1
+            if ql % 2 == 1 or c == CHUNKS - 1:
                 for bl in range(PACK):
                     nc.sync.dma_start(
-                        out=out_view[c, bl][:, (ql - 1) * WIDTH : (ql + 1) * WIDTH],
-                        in_=gx[bl:P:PACK, ql - 1 : ql + 1, :].rearrange("p ql k -> p (ql k)"),
+                        out=out_view[c, bl][:, first * WIDTH : (ql + 1) * WIDTH],
+                        in_=gx[bl:P:PACK, first : ql + 1, :].rearrange("p ql k -> p (ql k)"),
                     )
 
         def prepare(c, piece):
@@ -296,13 +308,15 @@ def tile_capsulelayer_t_v_kernel(tc, x, W, s, grad_out, out):
             if piece == 4:
                 dots(c, 0)
                 dots(c, 1)
+                factors_den(c)
             if piece == 5:
-                factors_of_q(c)
-                factors_of_dot(c)
+                factors_a(c)
 
         PIECES = 6
         LEAD = PIECES - PACK
         for piece in range(PIECES):
+            if piece == PIECES - 1:
+                factors_u(0)
             prepare(0, piece)
         turn_w()
         for piece in range(LEAD):
@@ -311,6 +325,10 @@ def tile_capsulelayer_t_v_kernel(tc, x, W, s, grad_out, out):
         for k in range(QUADS + 3):
             c = k // PACK
             ql = k % PACK
+            if c < CHUNKS and ql == 0:
+                factors_cf(c)
+            if c + 1 < CHUNKS and ql == PACK - 1:
+                factors_u(c + 1)
             if k < QUADS:
                 scaled_rows(c, ql)
             if c + 1 < CHUNKS:

@@ -62,10 +62,12 @@ def tile_capsulelayer_t_v_kernel(tc, x, W, s, grad_out, out):
                     nc.sync.dma_start(out=w_rows[t:P:PACK, :, :], in_=w_view[t])
             s_c = inputs.tile([P, CAPS_T, ROWS * COUT], F32, name="s_c")
             g_c = inputs.tile([P, CAPS_T, ROWS * COUT], BF16, name="g_c")
-            for t in range(PACK):
-                nc.sync.dma_start(out=s_c[t:P:PACK, :, :], in_=s_view[t, c])
-            for t in range(PACK):
-                nc.sync.dma_start(out=g_c[t:P:PACK, :, :], in_=g_view[t, c])
+            for n0 in range(0, CAPS_T, CAPS_T // 2):
+                caps = slice(n0, n0 + CAPS_T // 2)
+                for t in range(PACK):
+                    nc.sync.dma_start(out=s_c[t:P:PACK, caps, :], in_=s_view[t, c][:, caps, :])
+                for t in range(PACK):
+                    nc.sync.dma_start(out=g_c[t:P:PACK, caps, :], in_=g_view[t, c][:, caps, :])
             s_tiles.append(s_c)
             g_tiles.append(g_c)
 
@@ -303,11 +305,11 @@ def tile_capsulelayer_t_v_kernel(tc, x, W, s, grad_out, out):
                 square_bank(c, piece)
             if 1 <= piece <= BANKS:
                 sum_bank(c, piece - 1)
+            if 3 <= piece < 5:
+                dots(c, piece - 3)
             if 2 <= piece < 4:
                 products(c, piece - 2)
             if piece == 4:
-                dots(c, 0)
-                dots(c, 1)
                 factors_den(c)
             if piece == 5:
                 factors_a(c)

@@ -33,6 +33,23 @@ SUM_COLS = 64
 FLOPS = 2 * BATCH * CAPS * COUT * WIDTH
 BYTES = 2 * CAPS * WIDTH * COUT + 4 * CAPS * BATCH * COUT + 2 * CAPS * BATCH * COUT + 4 * BATCH * WIDTH
 
+LAG_TURN = 1
+LAG_ROUND = 2
+LAG_QUANT = 3
+LAG_MULT = 4
+LAG_OUT = 5
+LEAD_T = 11
+LEAD_SQ = 10
+LEAD_SUM = 9
+LEAD_ROOT = 5
+LEAD_PROD = 8
+LEAD_DOT = 6
+LEAD_DEN = 4
+LEAD_U = 3
+LEAD_A = 2
+LEAD_CF = 1
+W_STEP = -1
+
 
 def tile_capsulelayer_t_v_kernel(tc, x, W, s, grad_out, out):
     nc = tc.nc
@@ -57,19 +74,35 @@ def tile_capsulelayer_t_v_kernel(tc, x, W, s, grad_out, out):
         s_tiles = []
         g_tiles = []
         for c in range(CHUNKS):
-            if c == 1:
-                for t in range(PACK):
-                    nc.sync.dma_start(out=w_rows[t:P:PACK, :, :], in_=w_view[t])
             s_c = inputs.tile([P, CAPS_T, ROWS * COUT], F32, name="s_c")
             g_c = inputs.tile([P, CAPS_T, ROWS * COUT], BF16, name="g_c")
-            for n0 in range(0, CAPS_T, CAPS_T // 2):
-                caps = slice(n0, n0 + CAPS_T // 2)
-                for t in range(PACK):
-                    nc.sync.dma_start(out=s_c[t:P:PACK, caps, :], in_=s_view[t, c][:, caps, :])
-                for t in range(PACK):
-                    nc.sync.dma_start(out=g_c[t:P:PACK, caps, :], in_=g_view[t, c][:, caps, :])
             s_tiles.append(s_c)
             g_tiles.append(g_c)
+
+        def load_s(c, n0, n1):
+            for t in range(PACK):
+                nc.sync.dma_start(out=s_tiles[c][t:P:PACK, n0:n1, :], in_=s_view[t, c][:, n0:n1, :])
+
+        def load_g(c, n0, n1):
+            for t in range(PACK):
+                nc.sync.dma_start(out=g_tiles[c][t:P:PACK, n0:n1, :], in_=g_view[t, c][:, n0:n1, :])
+
+        def load_w():
+            for t in range(PACK):
+                nc.sync.dma_start(out=w_rows[t:P:PACK, :, :], in_=w_view[t])
+
+        HALF_CAPS = CAPS_T // 2
+        load_s(0, 0, HALF_CAPS)
+        load_g(0, 0, HALF_CAPS)
+        load_s(0, HALF_CAPS, CAPS_T)
+        load_g(0, HALF_CAPS, CAPS_T)
+        load_s(1, 0, CAPS_T)
+        load_g(1, 0, CAPS_T)
+        load_s(2, 0, CAPS_T)
+        load_w()
+        load_g(2, 0, CAPS_T)
+        load_s(3, 0, CAPS_T)
+        load_g(3, 0, CAPS_T)
 
         ident = const.tile([P, P], BF16)
         make_identity(nc, ident[:])
@@ -84,10 +117,10 @@ def tile_capsulelayer_t_v_kernel(tc, x, W, s, grad_out, out):
             op=ALU.add,
         )
 
-
+        q_psum_of = {}
         q_of = {}
+        turned_of = {}
         squared_of = {}
-        q_wide_of = {}
         root_of = {}
         gs_of = {}
         dot_of = {}
@@ -96,43 +129,51 @@ def tile_capsulelayer_t_v_kernel(tc, x, W, s, grad_out, out):
         neg_of = {}
         den_of = {}
         u_of = {}
+        r1_of = {}
         qd_of = {}
         terms_of = {}
+        ds_t_of = {}
         grouped_of = {}
+        codes_of = {}
         acc_of = {}
         gx_of = {}
         BLOCKS = 4
         BANKS = CAPS_T * ROWS * COUT // (BLOCKS * P)
+        HALF = PAIRS // 2
 
-        def square_bank(c, bank):
+        def turn_s(c, bank):
             s_flat = s_tiles[c][:].rearrange("p n f -> p (n f)")
             s_t = psum_bank.tile([P, BLOCKS, P], F32, tag="bank", name="s_t")
             for i in range(BLOCKS):
                 block = BLOCKS * bank + i
                 nc.tensor.transpose(out=s_t[:, i, :], in_=s_flat[:, block * P : (block + 1) * P], identity=ident_f32[:])
+            turned_of[(c, bank)] = s_t
+
+        def square(c, bank):
             sq_t = work.tile([P, BLOCKS, P], F32, name="sq_t", bufs=BANKS)
-            nc.scalar.activation(out=sq_t[:], in_=s_t[:], func=ACT.Square)
+            nc.scalar.activation(out=sq_t[:], in_=turned_of[(c, bank)][:], func=ACT.Square)
             squared_of[(c, bank)] = sq_t
 
         def sum_bank(c, bank):
             if bank == 0:
-                q_wide_of[c] = psum_q.tile([P, PAIRS + SUM_COLS - 8], F32, name="q_wide")
-                q_of[c] = q_wide_of[c][:, 0:PAIRS]
+                q_psum_of[c] = psum_q.tile([P, PAIRS + SUM_COLS - 8], F32, name="q_wide")
             for i in range(BLOCKS):
                 block = BLOCKS * bank + i
                 nc.tensor.matmul(
-                    out=q_wide_of[c][:, block * 8 : block * 8 + SUM_COLS],
+                    out=q_psum_of[c][:, block * 8 : block * 8 + SUM_COLS],
                     lhsT=squared_of[(c, bank)][:, i, :],
                     rhs=group_sum[:],
                     start=True,
                     stop=True,
                 )
-            if bank == BANKS - 1:
-                root = small.tile([P, PAIRS], F32, name="root")
-                nc.scalar.sqrt(out=root[:], in_=q_of[c])
-                root_of[c] = root
 
-        HALF = PAIRS // 2
+        def root(c):
+            r = small.tile([P, PAIRS], F32, name="root")
+            nc.scalar.sqrt(out=r[:], in_=q_psum_of[c][:, 0:PAIRS])
+            root_of[c] = r
+            q_sb = small.tile([P, PAIRS], F32, name="q_sb")
+            nc.scalar.copy(out=q_sb[:], in_=q_psum_of[c][:, 0:PAIRS])
+            q_of[c] = q_sb
 
         def products(c, half):
             if half == 0:
@@ -151,35 +192,43 @@ def tile_capsulelayer_t_v_kernel(tc, x, W, s, grad_out, out):
             pairs = slice(half * HALF, (half + 1) * HALF)
             nc.vector.tensor_reduce(out=dot_of[c][:, pairs], in_=gs_of[c][:, pairs, :], axis=AXIS.X, op=ALU.add)
 
-        def factors_den(c):
+        def f_den(c):
             den = small.tile([P, PAIRS], F32, name="den")
             nc.vector.scalar_tensor_tensor(
-                out=den[:], in0=q_of[c], scalar=1.0, in1=root_of[c][:], op0=ALU.add, op1=ALU.mult
+                out=den[:], in0=q_of[c][:], scalar=1.0, in1=root_of[c][:], op0=ALU.add, op1=ALU.mult
             )
             den_of[c] = den
 
-        def factors_u(c):
+        def f_u(c):
             u = small.tile([P, PAIRS], F32, name="u")
             nc.vector.reciprocal(out=u[:], in_=den_of[c][:])
+            u_of[c] = u
+
+        def f_qd(c):
             qd = small.tile([P, PAIRS], F32, name="qd")
             nc.vector.scalar_tensor_tensor(
-                out=qd[:], in0=q_of[c], scalar=1.0, in1=dot_of[c][:], op0=ALU.subtract, op1=ALU.mult
+                out=qd[:], in0=q_of[c][:], scalar=1.0, in1=dot_of[c][:], op0=ALU.subtract, op1=ALU.mult
             )
-            u_of[c] = u
             qd_of[c] = qd
 
-        def factors_a(c):
-            u = u_of[c]
+        def f_r1(c):
             r1 = small.tile([P, PAIRS], F32, name="r1")
-            nc.vector.tensor_tensor(out=r1[:], in0=u[:], in1=root_of[c][:], op=ALU.mult)
+            nc.vector.tensor_tensor(out=r1[:], in0=u_of[c][:], in1=root_of[c][:], op=ALU.mult)
+            r1_of[c] = r1
+
+        def f_a(c):
             a = small.tile([P, PAIRS], F32, name="a")
-            nc.vector.tensor_tensor(out=a[:], in0=q_of[c], in1=u[:], op=ALU.mult)
-            neg = small.tile([P, PAIRS], F32, name="neg")
-            nc.vector.scalar_tensor_tensor(out=neg[:], in0=u[:], scalar=-1.0, in1=r1[:], op0=ALU.mult, op1=ALU.mult)
+            nc.vector.tensor_tensor(out=a[:], in0=q_of[c][:], in1=u_of[c][:], op=ALU.mult)
             a_of[c] = a
+
+        def f_neg(c):
+            neg = small.tile([P, PAIRS], F32, name="neg")
+            nc.vector.scalar_tensor_tensor(
+                out=neg[:], in0=u_of[c][:], scalar=-1.0, in1=r1_of[c][:], op0=ALU.mult, op1=ALU.mult
+            )
             neg_of[c] = neg
 
-        def factors_cf(c):
+        def f_cf(c):
             cf = small.tile([P, PAIRS], F32, name="cf")
             nc.vector.tensor_tensor(out=cf[:], in0=neg_of[c][:], in1=qd_of[c][:], op=ALU.mult)
             cf_of[c] = cf
@@ -187,10 +236,11 @@ def tile_capsulelayer_t_v_kernel(tc, x, W, s, grad_out, out):
         w_grouped = const.tile([P, BS, KJ, PACK], BF16, align_bytes=64)
         w_codes = const.tile([P, WIDTH], U32, align_bytes=64)
         w_scales = const.tile([P, WIDTH], U8, align_bytes=64)
+        w_sorted = const.tile([P, KJ, CAPS_T, COUT], BF16)
         KJ_BANK = 8
+        w_t_of = {}
 
-        def turn_w():
-            w_sorted = const.tile([P, KJ, CAPS_T, COUT], BF16)
+        def sort_w():
             nc.scalar.copy(
                 out=w_sorted[:].rearrange("p kj n o -> p (kj n o)").bitcast(F32).rearrange(
                     "p (kj n w) -> p kj n w", kj=KJ, n=CAPS_T
@@ -199,18 +249,24 @@ def tile_capsulelayer_t_v_kernel(tc, x, W, s, grad_out, out):
                     "p (n kj w) -> p kj n w", n=CAPS_T, kj=KJ
                 ),
             )
-            for kj0 in range(0, KJ, KJ_BANK):
-                w_t = psum_bank.tile([P, KJ_BANK, P], BF16, tag="bank", name="w_t")
-                for i in range(KJ_BANK):
-                    nc.tensor.transpose(
-                        out=w_t[:, i, :],
-                        in_=w_sorted[:, kj0 + i, :, :].rearrange("p n o -> p (n o)"),
-                        identity=ident[:],
-                    )
-                nc.scalar.copy(
-                    out=w_grouped[:, :, kj0 : kj0 + KJ_BANK, :],
-                    in_=w_t[:].rearrange("p kj (ks t) -> p ks kj t", t=PACK),
+
+        def turn_w(i4):
+            kj0 = i4 * KJ_BANK
+            w_t = psum_acc.tile([P, KJ_BANK, P], BF16, tag="acc", name="w_t")
+            for i in range(KJ_BANK):
+                nc.tensor.transpose(
+                    out=w_t[:, i, :],
+                    in_=w_sorted[:, kj0 + i, :, :].rearrange("p n o -> p (n o)"),
+                    identity=ident[:],
                 )
+            w_t_of[i4] = w_t
+
+        def copy_w(i4):
+            kj0 = i4 * KJ_BANK
+            nc.scalar.copy(
+                out=w_grouped[:, :, kj0 : kj0 + KJ_BANK, :],
+                in_=w_t_of[i4][:].rearrange("p kj (ks t) -> p ks kj t", t=PACK),
+            )
 
         def quantise_w():
             nc.vector.quantize_mx(
@@ -219,30 +275,33 @@ def tile_capsulelayer_t_v_kernel(tc, x, W, s, grad_out, out):
                 in_=w_grouped[:].rearrange("p ks kj t -> p (ks kj t)"),
             )
 
-        def scaled_rows(c, ql):
-            s_rows = s_tiles[c][:].rearrange("p n (bl ql o) -> p ql n bl o", ql=PACK, o=COUT)[:, ql]
+        def scale_g(c, ql):
             g_rows = g_tiles[c][:].rearrange("p n (bl ql o) -> p ql n bl o", ql=PACK, o=COUT)[:, ql]
             a_rows = a_of[c][:].rearrange("p (n bl ql) -> p ql n bl", n=CAPS_T, ql=PACK)[:, ql]
-            cf_rows = cf_of[c][:].rearrange("p (n bl ql) -> p ql n bl", n=CAPS_T, ql=PACK)[:, ql]
-            shape = [P, CAPS_T, PACK, COUT]
-            ag = work.tile([P, PACK, CAPS_T, COUT], F32, name="ag")
+            ag = work.tile([P, PACK, CAPS_T, COUT], F32, name="ag", bufs=4)
             nc.vector.tensor_tensor(
                 out=ag[:].rearrange("p bl n o -> p n bl o"),
                 in0=g_rows,
-                in1=a_rows.unsqueeze(3).to_broadcast(shape),
+                in1=a_rows.unsqueeze(3).to_broadcast([P, CAPS_T, PACK, COUT]),
                 op=ALU.mult,
             )
-            cs = work.tile([P, PACK, CAPS_T, COUT], F32, name="cs")
+            terms_of[(c, ql, 0)] = ag
+
+        def scale_s(c, ql):
+            s_rows = s_tiles[c][:].rearrange("p n (bl ql o) -> p ql n bl o", ql=PACK, o=COUT)[:, ql]
+            cf_rows = cf_of[c][:].rearrange("p (n bl ql) -> p ql n bl", n=CAPS_T, ql=PACK)[:, ql]
+            cs = work.tile([P, PACK, CAPS_T, COUT], F32, name="cs", bufs=4)
             nc.vector.tensor_tensor(
                 out=cs[:].rearrange("p bl n o -> p n bl o"),
                 in0=s_rows,
-                in1=cf_rows.unsqueeze(3).to_broadcast(shape),
+                in1=cf_rows.unsqueeze(3).to_broadcast([P, CAPS_T, PACK, COUT]),
                 op=ALU.mult,
             )
-            terms_of[(c, ql)] = (ag, cs)
+            terms_of[(c, ql, 1)] = cs
 
         def turn(c, ql):
-            ag, cs = terms_of[(c, ql)]
+            ag = terms_of[(c, ql, 0)]
+            cs = terms_of[(c, ql, 1)]
             ds_t = psum_ds.tile([P, BS, PACK, PACK], F32, name="ds_t")
             for bl in range(PACK):
                 nc.tensor.matmul(
@@ -261,18 +320,25 @@ def tile_capsulelayer_t_v_kernel(tc, x, W, s, grad_out, out):
                     start=False,
                     stop=True,
                 )
+            ds_t_of[(c, ql)] = ds_t
+
+        def round_ds(c, ql):
             ds_grouped = work.tile([P, PACK * P], BF16, name="ds_grouped", align_bytes=64)
-            nc.scalar.copy(out=ds_grouped[:], in_=ds_t[:].rearrange("p bs bl t -> p (bs bl t)"))
+            nc.scalar.copy(out=ds_grouped[:], in_=ds_t_of[(c, ql)][:].rearrange("p bs bl t -> p (bs bl t)"))
             grouped_of[(c, ql)] = ds_grouped
 
-        def multiply(c, ql):
+        def quantise(c, ql):
             ds_codes = work.tile([P, P], U32, name="ds_codes", align_bytes=64)
             ds_scales = work.tile([P, P], U8, name="ds_scales", align_bytes=64)
             nc.vector.quantize_mx(out=ds_codes[:].bitcast(E5M2_X4), scales=ds_scales[:], in_=grouped_of[(c, ql)][:])
+            codes_of[(c, ql)] = (ds_codes, ds_scales)
+
+        def multiply(c, ql):
+            ds_codes, ds_scales = codes_of[(c, ql)]
             acc_of[(c, ql)] = []
             for k0 in range(0, WIDTH, N_MOVE):
                 cols = slice(k0, k0 + N_MOVE)
-                acc = psum_acc.tile([P, N_MOVE], F32, name="acc")
+                acc = psum_acc.tile([P, N_MOVE], F32, tag="acc", name="acc")
                 nc.tensor.matmul_mx(
                     out=acc[:],
                     lhsT=ds_codes[:].bitcast(E5M2_X4),
@@ -300,48 +366,73 @@ def tile_capsulelayer_t_v_kernel(tc, x, W, s, grad_out, out):
                         in_=gx[bl:P:PACK, first : ql + 1, :].rearrange("p ql k -> p (ql k)"),
                     )
 
-        def prepare(c, piece):
-            if piece < BANKS:
-                square_bank(c, piece)
-            if 1 <= piece <= BANKS:
-                sum_bank(c, piece - 1)
-            if 3 <= piece < 5:
-                dots(c, piece - 3)
-            if 2 <= piece < 4:
-                products(c, piece - 2)
-            if piece == 4:
-                factors_den(c)
-            if piece == 5:
-                factors_a(c)
-
-        PIECES = 6
-        LEAD = PIECES - PACK
-        for piece in range(PIECES):
-            if piece == PIECES - 1:
-                factors_u(0)
-            prepare(0, piece)
-        turn_w()
-        for piece in range(LEAD):
-            prepare(1, piece)
         QUADS = CHUNKS * PACK
-        for k in range(QUADS + 3):
-            c = k // PACK
-            ql = k % PACK
-            if c < CHUNKS and ql == 0:
-                factors_cf(c)
-            if c + 1 < CHUNKS and ql == PACK - 1:
-                factors_u(c + 1)
-            if k < QUADS:
-                scaled_rows(c, ql)
-            if c + 1 < CHUNKS:
-                prepare(c + 1, ql + LEAD)
-            if c + 2 < CHUNKS and ql >= PACK - LEAD:
-                prepare(c + 2, ql - (PACK - LEAD))
-            if 0 <= k - 3 < QUADS:
-                evacuate((k - 3) // PACK, (k - 3) % PACK)
-            if 0 <= k - 1 < QUADS:
-                turn((k - 1) // PACK, (k - 1) % PACK)
-            if k == 1:
+
+        def quad(k):
+            return (k // PACK, k % PACK)
+
+        for j in range(-LEAD_T, QUADS + LAG_OUT):
+            chunks = [(c, PACK * c - j) for c in range(CHUNKS)]
+            for c, ahead in chunks:
+                if ahead == LEAD_ROOT:
+                    root(c)
+            if 0 <= j - LAG_OUT < QUADS:
+                evacuate(*quad(j - LAG_OUT))
+            if 0 <= j - LAG_ROUND < QUADS:
+                round_ds(*quad(j - LAG_ROUND))
+            for c, ahead in chunks:
+                if 0 <= LEAD_SQ - ahead < BANKS:
+                    square(c, LEAD_SQ - ahead)
+            if j == W_STEP:
+                sort_w()
+            if j == W_STEP + 2:
+                for i4 in range(3):
+                    copy_w(i4)
+            if j == W_STEP + 3:
+                copy_w(3)
+            shorts = []
+            longs = []
+            for c, ahead in chunks:
+                if ahead == LEAD_DEN:
+                    shorts.append((f_den, c))
+                if ahead == LEAD_U:
+                    shorts.append((f_u, c))
+                    shorts.append((f_qd, c))
+                if ahead == LEAD_A:
+                    shorts.append((f_r1, c))
+                    shorts.append((f_a, c))
+                    shorts.append((f_neg, c))
+                if ahead == LEAD_CF:
+                    shorts.append((f_cf, c))
+            if 0 <= j < QUADS:
+                longs.append((scale_g,) + quad(j))
+                longs.append((scale_s,) + quad(j))
+            if 0 <= j - LAG_QUANT < QUADS:
+                longs.append((quantise,) + quad(j - LAG_QUANT))
+            for c, ahead in chunks:
+                if 0 <= LEAD_DOT - ahead < 2:
+                    longs.append((dots, c, LEAD_DOT - ahead))
+                if 0 <= LEAD_PROD - ahead < 2:
+                    longs.append((products, c, LEAD_PROD - ahead))
+            for i in range(max(len(shorts), len(longs))):
+                if i < len(shorts):
+                    shorts[i][0](*shorts[i][1:])
+                if i < len(longs):
+                    longs[i][0](*longs[i][1:])
+            if j == W_STEP + 4:
                 quantise_w()
-            if 0 <= k - 2 < QUADS:
-                multiply((k - 2) // PACK, (k - 2) % PACK)
+            if 0 <= j - LAG_TURN < QUADS:
+                turn(*quad(j - LAG_TURN))
+            for c, ahead in chunks:
+                if 0 <= LEAD_T - ahead < BANKS:
+                    turn_s(c, LEAD_T - ahead)
+            for c, ahead in chunks:
+                if 0 <= LEAD_SUM - ahead < BANKS:
+                    sum_bank(c, LEAD_SUM - ahead)
+            if j == W_STEP + 1:
+                for i4 in range(3):
+                    turn_w(i4)
+            if j == W_STEP + 2:
+                turn_w(3)
+            if 0 <= j - LAG_MULT < QUADS:
+                multiply(*quad(j - LAG_MULT))

from contextlib import ExitStack

import concourse.bass as bass
import concourse.mybir as mybir
import concourse.tile as tile
from concourse.masks import make_identity

F32 = mybir.dt.float32
BF16 = mybir.dt.bfloat16
U32 = mybir.dt.uint32
U8 = mybir.dt.uint8
E5M2_X4 = mybir.dt.float8_e5m2_x4
E4M3_X4 = mybir.dt.float8_e4m3fn_x4
ALU = mybir.AluOpType
ACT = mybir.ActivationFunctionType
AXIS = mybir.AxisListType

P = 128
PACK = 4
BATCH = 2048
CAPS = 32
COUT = 16
WIDTH = 1024
CAPS_T = CAPS // PACK
BS = P // PACK
CHUNKS = 4
ROWS = BATCH // BS // CHUNKS
PAIRS = CAPS_T * ROWS
KJ = WIDTH // BS
N_MOVE = 512
SUM_COLS = 64

FLOPS = 2 * BATCH * CAPS * COUT * WIDTH
BYTES = 2 * CAPS * WIDTH * COUT + 4 * CAPS * BATCH * COUT + 2 * CAPS * BATCH * COUT + 4 * BATCH * WIDTH

LAG_TURN = 1
LAG_ROUND = 2
LAG_QUANT = 3
LAG_MULT = 4
LAG_OUT = 5
LEAD_T = 11
LEAD_SQ = 10
LEAD_SUM = 9
LEAD_ROOT = 5
LEAD_PROD = 8
LEAD_DOT = 6
LEAD_DEN = 4
LEAD_U = 3
LEAD_A = 2
LEAD_CF = 1
W_STEP = -1


def tile_capsulelayer_t_v_kernel(tc, x, W, s, grad_out, out):
    nc = tc.nc
    s_view = s.rearrange("(t n) (bs c bq) o -> t c bs n (bq o)", t=PACK, bs=BS, c=CHUNKS)
    g_view = grad_out.rearrange("(t n) (bs c bq) x y o -> t c bs n (bq x y o)", t=PACK, bs=BS, c=CHUNKS)
    w_view = W.rearrange("(t n) (ks kr) i o -> t ks n (kr i o)", t=PACK, ks=BS)
    out_view = out.rearrange("(bs c bl ql) r i -> c bl bs (ql r i)", bs=BS, c=CHUNKS, bl=PACK)

    with ExitStack() as ctx:
        ctx.enter_context(tc.manual_schedule())
        const = ctx.enter_context(tc.tile_pool(name="const", bufs=1))
        inputs = ctx.enter_context(tc.tile_pool(name="inputs", bufs=CHUNKS))
        work = ctx.enter_context(tc.tile_pool(name="work", bufs=3))
        small = ctx.enter_context(tc.tile_pool(name="small", bufs=2))
        results = ctx.enter_context(tc.tile_pool(name="results", bufs=2))
        psum_bank = ctx.enter_context(tc.psum_pool(name="psum_bank", bufs=2))
        psum_q = ctx.enter_context(tc.psum_pool(name="psum_q", bufs=1))
        psum_ds = ctx.enter_context(tc.psum_pool(name="psum_ds", bufs=2))
        psum_acc = ctx.enter_context(tc.psum_pool(name="psum_acc", bufs=3))

        w_rows = const.tile([P, CAPS_T, KJ * COUT], BF16)
        s_tiles = []
        g_tiles = []
        for c in range(CHUNKS):
            s_c = inputs.tile([P, CAPS_T, ROWS * COUT], F32, name="s_c")
            g_c = inputs.tile([P, CAPS_T, ROWS * COUT], BF16, name="g_c")
            s_tiles.append(s_c)
            g_tiles.append(g_c)

        def load_s(c, n0, n1):
            for t in range(PACK):
                nc.sync.dma_start(out=s_tiles[c][t:P:PACK, n0:n1, :], in_=s_view[t, c][:, n0:n1, :])

        def load_g(c, n0, n1):
            for t in range(PACK):
                nc.sync.dma_start(out=g_tiles[c][t:P:PACK, n0:n1, :], in_=g_view[t, c][:, n0:n1, :])

        def load_w():
            for t in range(PACK):
                nc.sync.dma_start(out=w_rows[t:P:PACK, :, :], in_=w_view[t])

        HALF_CAPS = CAPS_T // 2
        load_s(0, 0, HALF_CAPS)
        load_g(0, 0, HALF_CAPS)
        load_s(0, HALF_CAPS, CAPS_T)
        load_g(0, HALF_CAPS, CAPS_T)
        load_s(1, 0, CAPS_T)
        load_g(1, 0, CAPS_T)
        load_s(2, 0, CAPS_T)
        load_w()
        load_g(2, 0, CAPS_T)
        load_s(3, 0, CAPS_T)
        load_g(3, 0, CAPS_T)

        ident = const.tile([P, P], BF16)
        make_identity(nc, ident[:])
        ident_f32 = const.tile([P, P], F32)
        make_identity(nc, ident_f32[:])
        group_sum = const.tile([P, SUM_COLS], F32)
        nc.vector.memset(group_sum[:], 0.0)
        nc.vector.tensor_reduce(
            out=group_sum[:, 0 : P // COUT],
            in_=ident_f32[:].rearrange("p (j o) -> p j o", o=COUT),
            axis=AXIS.X,
            op=ALU.add,
        )

        q_psum_of = {}
        q_of = {}
        turned_of = {}
        squared_of = {}
        root_of = {}
        gs_of = {}
        dot_of = {}
        a_of = {}
        cf_of = {}
        neg_of = {}
        den_of = {}
        u_of = {}
        r1_of = {}
        qd_of = {}
        terms_of = {}
        ds_t_of = {}
        grouped_of = {}
        codes_of = {}
        acc_of = {}
        gx_of = {}
        BLOCKS = 4
        BANKS = CAPS_T * ROWS * COUT // (BLOCKS * P)
        HALF = PAIRS // 2

        def turn_s(c, bank):
            s_flat = s_tiles[c][:].rearrange("p n f -> p (n f)")
            s_t = psum_bank.tile([P, BLOCKS, P], F32, tag="bank", name="s_t")
            for i in range(BLOCKS):
                block = BLOCKS * bank + i
                nc.tensor.transpose(out=s_t[:, i, :], in_=s_flat[:, block * P : (block + 1) * P], identity=ident_f32[:])
            turned_of[(c, bank)] = s_t

        def square(c, bank):
            sq_t = work.tile([P, BLOCKS, P], F32, name="sq_t", bufs=BANKS)
            nc.scalar.activation(out=sq_t[:], in_=turned_of[(c, bank)][:], func=ACT.Square)
            squared_of[(c, bank)] = sq_t

        def sum_bank(c, bank):
            if bank == 0:
                q_psum_of[c] = psum_q.tile([P, PAIRS + SUM_COLS - 8], F32, name="q_wide")
            for i in range(BLOCKS):
                block = BLOCKS * bank + i
                nc.tensor.matmul(
                    out=q_psum_of[c][:, block * 8 : block * 8 + SUM_COLS],
                    lhsT=squared_of[(c, bank)][:, i, :],
                    rhs=group_sum[:],
                    start=True,
                    stop=True,
                )

        def root(c):
            r = small.tile([P, PAIRS], F32, name="root")
            nc.scalar.sqrt(out=r[:], in_=q_psum_of[c][:, 0:PAIRS])
            root_of[c] = r
            q_sb = small.tile([P, PAIRS], F32, name="q_sb")
            nc.scalar.copy(out=q_sb[:], in_=q_psum_of[c][:, 0:PAIRS])
            q_of[c] = q_sb

        def products(c, half):
            if half == 0:
                gs_of[c] = work.tile([P, PAIRS, COUT], F32, name="gs", bufs=2)
            pairs = slice(half * HALF, (half + 1) * HALF)
            nc.vector.tensor_tensor(
                out=gs_of[c][:, pairs, :],
                in0=g_tiles[c][:].rearrange("p n (bq o) -> p (n bq) o", o=COUT)[:, pairs, :],
                in1=s_tiles[c][:].rearrange("p n (bq o) -> p (n bq) o", o=COUT)[:, pairs, :],
                op=ALU.mult,
            )

        def dots(c, half):
            if half == 0:
                dot_of[c] = small.tile([P, PAIRS], F32, name="dot")
            pairs = slice(half * HALF, (half + 1) * HALF)
            nc.vector.tensor_reduce(out=dot_of[c][:, pairs], in_=gs_of[c][:, pairs, :], axis=AXIS.X, op=ALU.add)

        def f_den(c):
            den = small.tile([P, PAIRS], F32, name="den")
            nc.vector.scalar_tensor_tensor(
                out=den[:], in0=q_of[c][:], scalar=1.0, in1=root_of[c][:], op0=ALU.add, op1=ALU.mult
            )
            den_of[c] = den

        def f_u(c):
            u = small.tile([P, PAIRS], F32, name="u")
            nc.vector.reciprocal(out=u[:], in_=den_of[c][:])
            u_of[c] = u

        def f_qd(c):
            qd = small.tile([P, PAIRS], F32, name="qd")
            nc.vector.scalar_tensor_tensor(
                out=qd[:], in0=q_of[c][:], scalar=1.0, in1=dot_of[c][:], op0=ALU.subtract, op1=ALU.mult
            )
            qd_of[c] = qd

        def f_r1(c):
            r1 = small.tile([P, PAIRS], F32, name="r1")
            nc.vector.tensor_tensor(out=r1[:], in0=u_of[c][:], in1=root_of[c][:], op=ALU.mult)
            r1_of[c] = r1

        def f_a(c):
            a = small.tile([P, PAIRS], F32, name="a")
            nc.vector.tensor_tensor(out=a[:], in0=q_of[c][:], in1=u_of[c][:], op=ALU.mult)
            a_of[c] = a

        def f_neg(c):
            neg = small.tile([P, PAIRS], F32, name="neg")
            nc.vector.scalar_tensor_tensor(
                out=neg[:], in0=u_of[c][:], scalar=-1.0, in1=r1_of[c][:], op0=ALU.mult, op1=ALU.mult
            )
            neg_of[c] = neg

        def f_cf(c):
            cf = small.tile([P, PAIRS], F32, name="cf")
            nc.vector.tensor_tensor(out=cf[:], in0=neg_of[c][:], in1=qd_of[c][:], op=ALU.mult)
            cf_of[c] = cf

        w_grouped = const.tile([P, BS, KJ, PACK], BF16, align_bytes=64)
        w_codes = const.tile([P, WIDTH], U32, align_bytes=64)
        w_scales = const.tile([P, WIDTH], U8, align_bytes=64)
        w_sorted = const.tile([P, KJ, CAPS_T, COUT], BF16)
        KJ_BANK = 8
        w_t_of = {}

        def sort_w():
            nc.scalar.copy(
                out=w_sorted[:].rearrange("p kj n o -> p (kj n o)").bitcast(F32).rearrange(
                    "p (kj n w) -> p kj n w", kj=KJ, n=CAPS_T
                ),
                in_=w_rows[:].rearrange("p n f -> p (n f)").bitcast(F32).rearrange(
                    "p (n kj w) -> p kj n w", n=CAPS_T, kj=KJ
                ),
            )

        def turn_w(i4):
            kj0 = i4 * KJ_BANK
            w_t = psum_acc.tile([P, KJ_BANK, P], BF16, tag="acc", name="w_t")
            for i in range(KJ_BANK):
                nc.tensor.transpose(
                    out=w_t[:, i, :],
                    in_=w_sorted[:, kj0 + i, :, :].rearrange("p n o -> p (n o)"),
                    identity=ident[:],
                )
            w_t_of[i4] = w_t

        def copy_w(i4):
            kj0 = i4 * KJ_BANK
            nc.scalar.copy(
                out=w_grouped[:, :, kj0 : kj0 + KJ_BANK, :],
                in_=w_t_of[i4][:].rearrange("p kj (ks t) -> p ks kj t", t=PACK),
            )

        def quantise_w():
            nc.vector.quantize_mx(
                out=w_codes[:].bitcast(E4M3_X4),
                scales=w_scales[:],
                in_=w_grouped[:].rearrange("p ks kj t -> p (ks kj t)"),
            )

        def scale_g(c, ql):
            g_rows = g_tiles[c][:].rearrange("p n (bl ql o) -> p ql n bl o", ql=PACK, o=COUT)[:, ql]
            a_rows = a_of[c][:].rearrange("p (n bl ql) -> p ql n bl", n=CAPS_T, ql=PACK)[:, ql]
            ag = work.tile([P, PACK, CAPS_T, COUT], F32, name="ag", bufs=4)
            nc.vector.tensor_tensor(
                out=ag[:].rearrange("p bl n o -> p n bl o"),
                in0=g_rows,
                in1=a_rows.unsqueeze(3).to_broadcast([P, CAPS_T, PACK, COUT]),
                op=ALU.mult,
            )
            terms_of[(c, ql, 0)] = ag

        def scale_s(c, ql):
            s_rows = s_tiles[c][:].rearrange("p n (bl ql o) -> p ql n bl o", ql=PACK, o=COUT)[:, ql]
            cf_rows = cf_of[c][:].rearrange("p (n bl ql) -> p ql n bl", n=CAPS_T, ql=PACK)[:, ql]
            cs = work.tile([P, PACK, CAPS_T, COUT], F32, name="cs", bufs=4)
            nc.vector.tensor_tensor(
                out=cs[:].rearrange("p bl n o -> p n bl o"),
                in0=s_rows,
                in1=cf_rows.unsqueeze(3).to_broadcast([P, CAPS_T, PACK, COUT]),
                op=ALU.mult,
            )
            terms_of[(c, ql, 1)] = cs

        def turn(c, ql):
            ag = terms_of[(c, ql, 0)]
            cs = terms_of[(c, ql, 1)]
            ds_t = psum_ds.tile([P, BS, PACK, PACK], F32, name="ds_t")
            for bl in range(PACK):
                nc.tensor.matmul(
                    out=ds_t[:, :, bl, :],
                    lhsT=ag[:, bl, :, :].rearrange("p n o -> p (n o)"),
                    rhs=ident_f32[:],
                    is_transpose=True,
                    start=True,
                    stop=False,
                )
                nc.tensor.matmul(
                    out=ds_t[:, :, bl, :],
                    lhsT=cs[:, bl, :, :].rearrange("p n o -> p (n o)"),
                    rhs=ident_f32[:],
                    is_transpose=True,
                    start=False,
                    stop=True,
                )
            ds_t_of[(c, ql)] = ds_t

        def round_ds(c, ql):
            ds_grouped = work.tile([P, PACK * P], BF16, name="ds_grouped", align_bytes=64)
            nc.scalar.copy(out=ds_grouped[:], in_=ds_t_of[(c, ql)][:].rearrange("p bs bl t -> p (bs bl t)"))
            grouped_of[(c, ql)] = ds_grouped

        def quantise(c, ql):
            ds_codes = work.tile([P, P], U32, name="ds_codes", align_bytes=64)
            ds_scales = work.tile([P, P], U8, name="ds_scales", align_bytes=64)
            nc.vector.quantize_mx(out=ds_codes[:].bitcast(E5M2_X4), scales=ds_scales[:], in_=grouped_of[(c, ql)][:])
            codes_of[(c, ql)] = (ds_codes, ds_scales)

        def multiply(c, ql):
            ds_codes, ds_scales = codes_of[(c, ql)]
            acc_of[(c, ql)] = []
            for k0 in range(0, WIDTH, N_MOVE):
                cols = slice(k0, k0 + N_MOVE)
                acc = psum_acc.tile([P, N_MOVE], F32, tag="acc", name="acc")
                nc.tensor.matmul_mx(
                    out=acc[:],
                    lhsT=ds_codes[:].bitcast(E5M2_X4),
                    lhsT_scale=ds_scales[:],
                    rhs=w_codes[:, cols].bitcast(E4M3_X4),
                    rhs_scale=w_scales[:, cols],
                    start=True,
                    stop=True,
                )
                acc_of[(c, ql)].append(acc)

        def evacuate(c, ql):
            if ql == 0:
                gx_of[c] = results.tile([P, PACK, WIDTH], F32, name="gx")
            gx = gx_of[c]
            for half in range(WIDTH // N_MOVE):
                cols = slice(half * N_MOVE, (half + 1) * N_MOVE)
                acc = acc_of[(c, ql)][half]
                nc.scalar.mul(out=gx[:, ql, cols], in_=acc[:], mul=1.0 / P)
            first = ql if c == CHUNKS - 1 else ql - 1
            if ql % 2 == 1 or c == CHUNKS - 1:
                for bl in range(PACK):
                    nc.sync.dma_start(
                        out=out_view[c, bl][:, first * WIDTH : (ql + 1) * WIDTH],
                        in_=gx[bl:P:PACK, first : ql + 1, :].rearrange("p ql k -> p (ql k)"),
                    )

        QUADS = CHUNKS * PACK

        def quad(k):
            return (k // PACK, k % PACK)

        for j in range(-LEAD_T, QUADS + LAG_OUT):
            chunks = [(c, PACK * c - j) for c in range(CHUNKS)]
            for c, ahead in chunks:
                if ahead == LEAD_ROOT:
                    root(c)
            if 0 <= j - LAG_OUT < QUADS:
                evacuate(*quad(j - LAG_OUT))
            if 0 <= j - LAG_ROUND < QUADS:
                round_ds(*quad(j - LAG_ROUND))
            for c, ahead in chunks:
                if 0 <= LEAD_SQ - ahead < BANKS:
                    square(c, LEAD_SQ - ahead)
            if j == W_STEP:
                sort_w()
            if j == W_STEP + 2:
                for i4 in range(3):
                    copy_w(i4)
            if j == W_STEP + 3:
                copy_w(3)
            shorts = []
            longs = []
            for c, ahead in chunks:
                if ahead == LEAD_DEN:
                    shorts.append((f_den, c))
                if ahead == LEAD_U:
                    shorts.append((f_u, c))
                    shorts.append((f_qd, c))
                if ahead == LEAD_A:
                    shorts.append((f_r1, c))
                    shorts.append((f_a, c))
                    shorts.append((f_neg, c))
                if ahead == LEAD_CF:
                    shorts.append((f_cf, c))
            if 0 <= j < QUADS:
                longs.append((scale_g,) + quad(j))
                longs.append((scale_s,) + quad(j))
            if 0 <= j - LAG_QUANT < QUADS:
                longs.append((quantise,) + quad(j - LAG_QUANT))
            for c, ahead in chunks:
                if 0 <= LEAD_DOT - ahead < 2:
                    longs.append((dots, c, LEAD_DOT - ahead))
                if 0 <= LEAD_PROD - ahead < 2:
                    longs.append((products, c, LEAD_PROD - ahead))
            for i in range(max(len(shorts), len(longs))):
                if i < len(shorts):
                    shorts[i][0](*shorts[i][1:])
                if i < len(longs):
                    longs[i][0](*longs[i][1:])
            if j == W_STEP + 4:
                quantise_w()
            if 0 <= j - LAG_TURN < QUADS:
                turn(*quad(j - LAG_TURN))
            for c, ahead in chunks:
                if 0 <= LEAD_T - ahead < BANKS:
                    turn_s(c, LEAD_T - ahead)
            for c, ahead in chunks:
                if 0 <= LEAD_SUM - ahead < BANKS:
                    sum_bank(c, LEAD_SUM - ahead)
            if j == W_STEP + 1:
                for i4 in range(3):
                    turn_w(i4)
            if j == W_STEP + 2:
                turn_w(3)
            if 0 <= j - LAG_MULT < QUADS:
                multiply(*quad(j - LAG_MULT))
